import numpy as np
import ml_dtypes


def mxq(x, axis, fmt="e4m3"):
    dtype, down = {"e4m3": (ml_dtypes.float8_e4m3fn, 7), "e5m2": (ml_dtypes.float8_e5m2, 14)}[fmt]
    v = np.moveaxis(np.asarray(x, np.float32).astype(ml_dtypes.bfloat16).astype(np.float64), axis, -1)
    blocks = v.reshape(v.shape[:-1] + (-1, 32))
    amax = np.abs(blocks).max(-1, keepdims=True)
    byte = np.maximum(np.where(amax > 0, np.frexp(amax)[1] - 1 + 127, 0) - down, 1)
    scale = np.exp2(byte - 127.0)
    codes = (blocks / scale).astype(np.float32).astype(dtype).astype(np.float64)
    return np.moveaxis((codes * scale).reshape(v.shape), -1, axis)


WIDE = False


def mx_kscale(k):
    if not WIDE:
        return np.ones(k)
    levels = np.array([10, -10, 5, -5, 0])
    if k % 512:
        return np.exp2(np.random.permutation(np.resize(levels, k // 32))).repeat(32)
    a = np.empty((k // 512, 16))
    for p in range(k // 512):
        a[p, :8] = np.random.permutation(np.resize(levels, 8))
        for g in range(8):
            far = levels[np.abs(levels - a[p, g]) >= 10]
            a[p, g + 8] = far[np.random.randint(len(far))]
    return np.exp2(a.ravel()).repeat(32)


BF16 = ml_dtypes.bfloat16


def bf(x):
    return np.asarray(x, np.float32).astype(BF16)


def f64(x):
    return np.asarray(x).astype(np.float64)


T, M, HW, D, DK, H = 2, 512, 768, 1024, 1024, 8
EPS = 1e-6
EXTENT = 27.0


def rope_2d(x, pos):
    nt, n, c = x.shape
    half, quarter = c // 2, c // 4
    theta = 100.0 ** (-2.0 * np.arange(quarter) / half)

    def apply(part, p):
        fr = p[..., None] * theta
        cos, sin = np.cos(fr), np.sin(fr)
        pr = part.reshape(nt, n, quarter, 2)
        x1, x2 = pr[..., 0], pr[..., 1]
        return np.stack([x1 * cos - x2 * sin, x1 * sin + x2 * cos], axis=-1).reshape(nt, n, half)

    return np.concatenate([apply(x[:, :, :half], pos[..., 0]), apply(x[:, :, half:], pos[..., 1])], axis=-1)


def layernorm_nobias(x, gamma):
    mu = x.mean(-1, keepdims=True)
    var = ((x - mu) ** 2).mean(-1, keepdims=True)
    return (x - mu) / np.sqrt(var + EPS) * gamma


def setup_inputs():
    s = mx_kscale(D)
    return {"updated_track_tokens": bf(np.random.standard_normal((T, M, D)) * s),
            "tracks": bf(np.random.uniform(0.0, EXTENT, (T, M, 2))),
            "W_k": bf(np.random.standard_normal((DK, D)) / np.sqrt(D) / s),
            "k_gamma": bf(1.0 + 0.1 * np.random.standard_normal(DK))}


def reference(updated_track_tokens, tracks, W_k, k_gamma):
    k = mxq(f64(updated_track_tokens), 2, "e4m3") @ mxq(f64(W_k), 1, "e4m3").T
    k = rope_2d(k, f64(tracks))
    return layernorm_nobias(k, f64(k_gamma))

@@ -1,0 +1,265 @@
+import math
+from contextlib import ExitStack
+
+import concourse.mybir as mybir
+from concourse.masks import make_identity
+
+F32 = mybir.dt.float32
+BF16 = mybir.dt.bfloat16
+U32 = mybir.dt.uint32
+U8 = mybir.dt.uint8
+FP8X4 = mybir.dt.float8_e4m3fn_x4
+ALU = mybir.AluOpType
+ACT = mybir.ActivationFunctionType
+
+P = 128
+TOKENS = 1024
+D = 1024
+CHANNELS = 1024
+TILES = TOKENS // P
+K_PASS = 4 * P
+PASSES = D // K_PASS
+HALF = CHANNELS // 2
+PAIRS = HALF // 2
+DOUBLINGS = 8
+assert 2**DOUBLINGS == PAIRS
+W_BLOCKS = CHANNELS // (2 * P)
+WORDS = D // 2
+EPS = 1e-6
+THETA_BASE = 100.0
+TWO_PI = 2.0 * math.pi
+ROUND_MAGIC = 1.5 * 2.0**23
+
+FLOPS = 2 * TOKENS * D * CHANNELS
+
+
+def tile_attentionalsplatting_pa_kernel(tc, updated_track_tokens, tracks, W_k, k_gamma, out):
+    nc = tc.nc
+
+    x_dram = updated_track_tokens.flatten_outer_dims().rearrange("(p j) k -> p j k", j=TILES)
+    pos_dram = tracks.flatten_outer_dims().rearrange("(p j) c -> p (j c)", j=TILES)
+    w_dram = W_k.rearrange("(q p e) k -> q p (e k)", q=W_BLOCKS, p=P, e=2)
+    out_dram = out.flatten_outer_dims().rearrange("(p j) c -> p j c", j=TILES)
+
+    with ExitStack() as ctx:
+        keep = ctx.enter_context(tc.tile_pool(name="keep", bufs=1))
+        double = ctx.enter_context(tc.tile_pool(name="double", bufs=2))
+        triple = ctx.enter_context(tc.tile_pool(name="triple", bufs=3))
+        stats = ctx.enter_context(tc.tile_pool(name="stats", bufs=4))
+        flip_banks = ctx.enter_context(tc.psum_pool(name="flip_banks", bufs=4))
+        key_banks = ctx.enter_context(tc.psum_pool(name="key_banks", bufs=2))
+        ctx.enter_context(tc.manual_schedule())
+
+        pos_bf = keep.tile([P, 2 * TILES], BF16)
+        nc.sync.dma_start(out=pos_bf[:], in_=pos_dram)
+        w_raw = keep.tile([P, W_BLOCKS, 2, D], BF16)
+        for q in range(W_BLOCKS):
+            nc.sync.dma_start(out=w_raw[:, q].rearrange("p e k -> p (e k)"), in_=w_dram[q])
+        x_raw = keep.tile([P, TILES, D], BF16)
+        for j in range(0, TILES, 2):
+            nc.sync.dma_start(out=x_raw[:, j : j + 2, :], in_=x_dram[:, j : j + 2, :])
+        gamma_bf = keep.tile([P, CHANNELS], BF16)
+        nc.sync.dma_start(out=gamma_bf[:], in_=k_gamma.partition_broadcast(P))
+
+        ident = keep.tile([P, P], F32)
+        make_identity(nc, ident[:])
+        minus_half = keep.tile([P, 1], F32)
+        nc.vector.memset(minus_half[:], -0.5)
+        theta = keep.tile([P, PAIRS], F32)
+        nc.vector.memset(theta[:, 0:1], 1.0)
+        for w in [2**doubling for doubling in range(DOUBLINGS)]:
+            nc.vector.tensor_scalar_mul(
+                out=theta[:, w : 2 * w], in0=theta[:, 0:w], scalar1=THETA_BASE ** (-w / PAIRS)
+            )
+        pos = keep.tile([P, 2 * TILES], F32)
+        nc.vector.tensor_copy(out=pos[:], in_=pos_bf[:])
+        gamma = keep.tile([P, CHANNELS], F32)
+        turns = keep.tile([P, 2 * TILES, PAIRS], F32)
+
+        w_grouped = keep.tile([P, 2, PASSES * HALF * 4], BF16, align_bytes=64)
+        w_codes = keep.tile([P, 2, PASSES * HALF], U32, align_bytes=64)
+        w_scales = keep.tile([P, 2, PASSES * HALF], U8, align_bytes=64)
+        x_grouped = keep.tile([P, TILES, PASSES * P * 4], BF16, align_bytes=64)
+        x_codes = keep.tile([P, TILES, PASSES * P], U32, align_bytes=64)
+        x_scales = keep.tile([P, TILES, PASSES * P], U8, align_bytes=64)
+
+        frac_of, trig_of, keys_of, rotated_of, minus_mean_of = {}, {}, {}, {}, {}
+        sum_squares_of, rstd_of, shift_of, normed_of = {}, {}, {}, {}
+
+        def flip_rows(words, grouped_words, copy_engine):
+            bank = flip_banks.tile([P, PASSES * 2 * P], F32, name="flip_bank")
+            for t in range(PASSES * 2):
+                g, u = divmod(t, 2)
+                every_second = words[:, g * 2 * P + u : (g + 1) * 2 * P : 2]
+                nc.tensor.transpose(bank[:, t * P : (t + 1) * P], every_second, ident[:])
+            planes = bank[:].rearrange("p (g u r) -> p g r u", g=PASSES, u=2)
+            if copy_engine == "scalar":
+                nc.scalar.copy(out=grouped_words, in_=planes)
+            else:
+                nc.vector.tensor_copy(out=grouped_words, in_=planes)
+
+        def flip_weights(q):
+            h, b = divmod(q, W_BLOCKS // 2)
+            half_words = w_grouped[:, h, :].bitcast(F32).rearrange("p (g c u) -> p g c u", g=PASSES, u=2)
+            for e, copy_engine in enumerate(["scalar", "vector"]):
+                first = e * PAIRS + b * P
+                flip_rows(w_raw[:, q, e, :].bitcast(F32), half_words[:, :, first : first + P, :], copy_engine)
+
+        def quantise_weights(h):
+            nc.vector.quantize_mx(
+                out=w_codes[:, h, :].bitcast(FP8X4), scales=w_scales[:, h, :], in_=w_grouped[:, h, :]
+            )
+
+        def flip_tokens(j):
+            tile_words = x_grouped[:, j, :].bitcast(F32).rearrange("p (g r u) -> p g r u", g=PASSES, u=2)
+            flip_rows(x_raw[:, j, :].bitcast(F32), tile_words, "scalar")
+
+        def quantise_tokens(j):
+            nc.vector.quantize_mx(
+                out=x_codes[:, j, :].bitcast(FP8X4), scales=x_scales[:, j, :], in_=x_grouped[:, j, :]
+            )
+
+        def angles_in_turns(engine, pair):
+            for column in range(4 * pair, 4 * pair + 4):
+                engine.tensor_scalar(
+                    out=turns[:, column, :],
+                    in0=theta[:],
+                    scalar1=pos[:, column : column + 1],
+                    scalar2=1.0 / TWO_PI,
+                    op0=ALU.mult,
+                    op1=ALU.mult,
+                )
+
+        def reduce_angles(pair):
+            pair_turns = turns[:, 4 * pair : 4 * pair + 4, :]
+            whole = keep.tile([P, 4, PAIRS], F32, name="whole")
+            nc.vector.tensor_scalar(
+                out=whole[:], in0=pair_turns, scalar1=ROUND_MAGIC, scalar2=ROUND_MAGIC, op0=ALU.add, op1=ALU.subtract
+            )
+            frac = double.tile([P, 2, HALF], F32, name="frac")
+            nc.vector.tensor_sub(
+                out=frac[:].rearrange("p t (h i) -> p (t h) i", h=2), in0=pair_turns, in1=whole[:]
+            )
+            frac_of[pair] = frac
+            trig_of[pair] = double.tile([P, 2, 2, HALF], F32, name="trig")
+
+        def cos_and_sin(j):
+            frac = frac_of[j // 2][:, j % 2, :]
+            trig = trig_of[j // 2][:, j % 2]
+            nc.scalar.activation(out=trig[:, 1, :], in_=frac, func=ACT.Sin, scale=TWO_PI)
+            abs_frac = double.tile([P, HALF], F32, name="abs_frac")
+            nc.scalar.activation(out=abs_frac[:], in_=frac, func=ACT.Abs)
+            nc.scalar.activation(out=trig[:, 0, :], in_=abs_frac[:], func=ACT.Sin, scale=-TWO_PI, bias=math.pi / 2.0)
+
+        def project(j):
+            keys_of[j] = []
+            for h in range(2):
+                bank = key_banks.tile([P, HALF], F32, name="key_bank_%d" % h)
+                for g in range(PASSES):
+                    nc.tensor.matmul_mx(
+                        out=bank[:],
+                        lhsT=x_codes[:, j, g * P : (g + 1) * P].bitcast(FP8X4),
+                        lhsT_scale=x_scales[:, j, g * P : (g + 1) * P],
+                        rhs=w_codes[:, h, g * HALF : (g + 1) * HALF].bitcast(FP8X4),
+                        rhs_scale=w_scales[:, h, g * HALF : (g + 1) * HALF],
+                        start=(g == 0),
+                        stop=(g == PASSES - 1),
+                    )
+                keys_of[j].append(bank)
+
+        def rotate(j):
+            trig = trig_of[j // 2][:, j % 2]
+            products = double.tile([P, 2, 2, 2, PAIRS], F32, name="products")
+            for h in range(2):
+                planes = keys_of[j][h][:].rearrange("p (e i) -> p e i", e=2)
+                nc.vector.tensor_mul(
+                    out=products[:, h],
+                    in0=planes.unsqueeze(1).to_broadcast([P, 2, 2, PAIRS]),
+                    in1=trig[:, :, h * PAIRS : (h + 1) * PAIRS].unsqueeze(2).to_broadcast([P, 2, 2, PAIRS]),
+                )
+            rotated = triple.tile([P, 2, 2, PAIRS], F32, name="rotated")
+            sums = stats.tile([P, 2], F32, name="sums")
+            nc.vector.scalar_tensor_tensor(
+                out=rotated[:, :, 0, :], in0=products[:, :, 0, 0, :], scalar=1.0, in1=products[:, :, 1, 1, :],
+                op0=ALU.mult, op1=ALU.subtract, accum_out=sums[:, 0:1],
+            )
+            nc.vector.scalar_tensor_tensor(
+                out=rotated[:, :, 1, :], in0=products[:, :, 0, 1, :], scalar=1.0, in1=products[:, :, 1, 0, :],
+                op0=ALU.mult, op1=ALU.add, accum_out=sums[:, 1:2],
+            )
+            minus_mean = stats.tile([P, 1], F32, name="minus_mean")
+            nc.vector.tensor_scalar(
+                out=minus_mean[:], in0=sums[:, 0:1], scalar1=sums[:, 1:2], scalar2=-1.0 / CHANNELS,
+                op0=ALU.add, op1=ALU.mult,
+            )
+            rotated_of[j], minus_mean_of[j] = rotated, minus_mean
+
+        def sum_of_squares(j):
+            squares = double.tile([P, CHANNELS], F32, name="squares")
+            sum_squares_of[j] = stats.tile([P, 1], F32, name="sum_squares")
+            nc.scalar.activation(
+                out=squares[:], in_=rotated_of[j][:].rearrange("p h e i -> p (h e i)"), func=ACT.Square,
+                bias=minus_mean_of[j][:], scale=1.0, accum_out=sum_squares_of[j][:],
+            )
+
+        def scale_and_shift(j):
+            var_eps = stats.tile([P, 1], F32, name="var_eps")
+            nc.gpsimd.tensor_scalar(
+                out=var_eps[:], in0=sum_squares_of[j][:], scalar1=1.0 / CHANNELS, scalar2=EPS,
+                op0=ALU.mult, op1=ALU.add,
+            )
+            rstd_of[j] = stats.tile([P, 1], F32, name="rstd")
+            nc.gpsimd.tensor_tensor(out=rstd_of[j][:], in0=var_eps[:], in1=minus_half[:], op=ALU.pow)
+            shift_of[j] = stats.tile([P, 1], F32, name="shift")
+            nc.gpsimd.tensor_tensor(out=shift_of[j][:], in0=minus_mean_of[j][:], in1=rstd_of[j][:], op=ALU.mult)
+
+        def normalise(j):
+            normed_of[j] = double.tile([P, CHANNELS], F32, name="normed")
+            nc.scalar.activation(
+                out=normed_of[j][:].rearrange("p (h i e) -> p h i e", h=2, e=2),
+                in_=rotated_of[j][:].rearrange("p h e i -> p h i e"),
+                func=ACT.Identity, bias=shift_of[j][:], scale=rstd_of[j][:],
+            )
+
+        def apply_gamma_and_store(j):
+            engine = nc.vector if j == TILES - 1 else nc.gpsimd
+            result = triple.tile([P, CHANNELS], F32, name="result")
+            engine.tensor_tensor(out=result[:], in0=normed_of[j][:], in1=gamma[:], op=ALU.mult)
+            nc.sync.dma_start(out=out_dram[:, j, :], in_=result[:])
+
+        angles_in_turns(nc.vector, 0)
+        for pair in range(1, TILES // 2):
+            angles_in_turns(nc.gpsimd, pair)
+        reduce_angles(0)
+        for q in range(W_BLOCKS):
+            flip_weights(q)
+            if q % 2 == 1:
+                quantise_weights(q // 2)
+        flip_tokens(0)
+        cos_and_sin(0)
+        flip_tokens(1)
+        quantise_tokens(0)
+        project(0)
+        reduce_angles(1)
+        cos_and_sin(1)
+        nc.gpsimd.tensor_scalar(out=gamma[:], in0=gamma_bf[:], scalar1=1.0, scalar2=0.0, op0=ALU.mult, op1=ALU.add)
+
+        for s in range(TILES + 2):
+            if s + 2 < TILES:
+                flip_tokens(s + 2)
+            if s + 1 < TILES:
+                quantise_tokens(s + 1)
+                project(s + 1)
+            if 1 <= s <= TILES:
+                scale_and_shift(s - 1)
+            if s + 2 < TILES:
+                cos_and_sin(s + 2)
+            if 1 <= s <= TILES:
+                normalise(s - 1)
+            if s >= 2:
+                apply_gamma_and_store(s - 2)
+            if s < TILES:
+                rotate(s)
+                if s % 2 == 1 and s + 3 < TILES:
+                    reduce_angles((s + 3) // 2)
+                sum_of_squares(s)

@@ -8,6 +8,7 @@ F32 = mybir.dt.float32
 BF16 = mybir.dt.bfloat16
 U32 = mybir.dt.uint32
 U8 = mybir.dt.uint8
+I32 = mybir.dt.int32
 FP8X4 = mybir.dt.float8_e4m3fn_x4
 ALU = mybir.AluOpType
 ACT = mybir.ActivationFunctionType
@@ -28,7 +29,9 @@ WORDS = D // 2
 EPS = 1e-6
 THETA_BASE = 100.0
 TWO_PI = 2.0 * math.pi
-ROUND_MAGIC = 1.5 * 2.0**23
+ROOT_CHANNELS = math.sqrt(CHANNELS)
+GAMMA_ON_GPSIMD = {3: 0, 4: 1, 5: 2, 6: 3}
+GAMMA_ON_VECTOR = {6: 4, 7: 5}
 
 FLOPS = 2 * TOKENS * D * CHANNELS
 
@@ -45,6 +48,7 @@ def tile_attentionalsplatting_pa_kernel(tc, updated_track_tokens, tracks, W_k, k
         keep = ctx.enter_context(tc.tile_pool(name="keep", bufs=1))
         double = ctx.enter_context(tc.tile_pool(name="double", bufs=2))
         triple = ctx.enter_context(tc.tile_pool(name="triple", bufs=3))
+        quad = ctx.enter_context(tc.tile_pool(name="quad", bufs=4))
         stats = ctx.enter_context(tc.tile_pool(name="stats", bufs=4))
         flip_banks = ctx.enter_context(tc.psum_pool(name="flip_banks", bufs=4))
         key_banks = ctx.enter_context(tc.psum_pool(name="key_banks", bufs=2))
@@ -53,20 +57,32 @@ def tile_attentionalsplatting_pa_kernel(tc, updated_track_tokens, tracks, W_k, k
         pos_bf = keep.tile([P, 2 * TILES], BF16)
         nc.sync.dma_start(out=pos_bf[:], in_=pos_dram)
         w_raw = keep.tile([P, W_BLOCKS, 2, D], BF16)
-        for q in range(W_BLOCKS):
-            nc.sync.dma_start(out=w_raw[:, q].rearrange("p e k -> p (e k)"), in_=w_dram[q])
         x_raw = keep.tile([P, TILES, D], BF16)
-        for j in range(0, TILES, 2):
+
+        def load_weights(q):
+            nc.sync.dma_start(out=w_raw[:, q].rearrange("p e k -> p (e k)"), in_=w_dram[q])
+
+        def load_tokens(j):
             nc.sync.dma_start(out=x_raw[:, j : j + 2, :], in_=x_dram[:, j : j + 2, :])
+
+        load_weights(0)
+        load_weights(1)
+        load_tokens(0)
+        load_weights(2)
+        load_weights(3)
+        for j in range(2, TILES, 2):
+            load_tokens(j)
         gamma_bf = keep.tile([P, CHANNELS], BF16)
         nc.sync.dma_start(out=gamma_bf[:], in_=k_gamma.partition_broadcast(P))
 
         ident = keep.tile([P, P], F32)
         make_identity(nc, ident[:])
         minus_half = keep.tile([P, 1], F32)
-        nc.vector.memset(minus_half[:], -0.5)
+        nc.gpsimd.memset(minus_half[:], -0.5)
         theta = keep.tile([P, PAIRS], F32)
-        nc.vector.memset(theta[:, 0:1], 1.0)
+        one = keep.tile([P, 1], F32)
+        nc.vector.memset(one[:], 1.0)
+        nc.vector.tensor_scalar_mul(out=theta[:, 0:1], in0=one[:], scalar1=1.0 / TWO_PI)
         for w in [2**doubling for doubling in range(DOUBLINGS)]:
             nc.vector.tensor_scalar_mul(
                 out=theta[:, w : 2 * w], in0=theta[:, 0:w], scalar1=THETA_BASE ** (-w / PAIRS)
@@ -74,7 +90,8 @@ def tile_attentionalsplatting_pa_kernel(tc, updated_track_tokens, tracks, W_k, k
         pos = keep.tile([P, 2 * TILES], F32)
         nc.vector.tensor_copy(out=pos[:], in_=pos_bf[:])
         gamma = keep.tile([P, CHANNELS], F32)
-        turns = keep.tile([P, 2 * TILES, PAIRS], F32)
+        whole = keep.tile([P, 2 * TILES, PAIRS], I32)
+        frac = keep.tile([P, 2 * TILES, PAIRS], F32)
 
         w_grouped = keep.tile([P, 2, PASSES * HALF * 4], BF16, align_bytes=64)
         w_codes = keep.tile([P, 2, PASSES * HALF], U32, align_bytes=64)
@@ -83,7 +100,7 @@ def tile_attentionalsplatting_pa_kernel(tc, updated_track_tokens, tracks, W_k, k
         x_codes = keep.tile([P, TILES, PASSES * P], U32, align_bytes=64)
         x_scales = keep.tile([P, TILES, PASSES * P], U8, align_bytes=64)
 
-        frac_of, trig_of, keys_of, rotated_of, minus_mean_of = {}, {}, {}, {}, {}
+        trig_of, keys_of, products_of, rotated_of, sums_of, minus_mean_of = {}, {}, {}, {}, {}, {}
         sum_squares_of, rstd_of, shift_of, normed_of = {}, {}, {}, {}
 
         def flip_rows(words, grouped_words, copy_engine):
@@ -110,89 +127,82 @@ def tile_attentionalsplatting_pa_kernel(tc, updated_track_tokens, tracks, W_k, k
                 out=w_codes[:, h, :].bitcast(FP8X4), scales=w_scales[:, h, :], in_=w_grouped[:, h, :]
             )
 
-        def flip_tokens(j):
+        def flip_tokens(j, copy_engine):
             tile_words = x_grouped[:, j, :].bitcast(F32).rearrange("p (g r u) -> p g r u", g=PASSES, u=2)
-            flip_rows(x_raw[:, j, :].bitcast(F32), tile_words, "scalar")
+            flip_rows(x_raw[:, j, :].bitcast(F32), tile_words, copy_engine)
 
         def quantise_tokens(j):
             nc.vector.quantize_mx(
                 out=x_codes[:, j, :].bitcast(FP8X4), scales=x_scales[:, j, :], in_=x_grouped[:, j, :]
             )
 
-        def angles_in_turns(engine, pair):
-            for column in range(4 * pair, 4 * pair + 4):
-                engine.tensor_scalar(
-                    out=turns[:, column, :],
-                    in0=theta[:],
-                    scalar1=pos[:, column : column + 1],
-                    scalar2=1.0 / TWO_PI,
-                    op0=ALU.mult,
-                    op1=ALU.mult,
+        def whole_turns(j):
+            for column in (2 * j, 2 * j + 1):
+                nc.gpsimd.tensor_scalar(
+                    out=whole[:, column, :], in0=theta[:], scalar1=pos[:, column : column + 1], scalar2=0.0,
+                    op0=ALU.mult, op1=ALU.add,
                 )
 
-        def reduce_angles(pair):
-            pair_turns = turns[:, 4 * pair : 4 * pair + 4, :]
-            whole = keep.tile([P, 4, PAIRS], F32, name="whole")
-            nc.vector.tensor_scalar(
-                out=whole[:], in0=pair_turns, scalar1=ROUND_MAGIC, scalar2=ROUND_MAGIC, op0=ALU.add, op1=ALU.subtract
-            )
-            frac = double.tile([P, 2, HALF], F32, name="frac")
-            nc.vector.tensor_sub(
-                out=frac[:].rearrange("p t (h i) -> p (t h) i", h=2), in0=pair_turns, in1=whole[:]
-            )
-            frac_of[pair] = frac
-            trig_of[pair] = double.tile([P, 2, 2, HALF], F32, name="trig")
+        def reduce_angles(j):
+            for column in (2 * j, 2 * j + 1):
+                nc.vector.scalar_tensor_tensor(
+                    out=frac[:, column, :], in0=theta[:], scalar=pos[:, column : column + 1],
+                    in1=whole[:, column, :], op0=ALU.mult, op1=ALU.subtract,
+                )
 
         def cos_and_sin(j):
-            frac = frac_of[j // 2][:, j % 2, :]
-            trig = trig_of[j // 2][:, j % 2]
-            nc.scalar.activation(out=trig[:, 1, :], in_=frac, func=ACT.Sin, scale=TWO_PI)
+            tile_frac = frac[:, 2 * j : 2 * j + 2, :].rearrange("p h i -> p (h i)")
+            trig_of[j] = quad.tile([P, 2, HALF], F32, name="trig")
+            nc.scalar.activation(out=trig_of[j][:, 1, :], in_=tile_frac, func=ACT.Sin, scale=TWO_PI)
             abs_frac = double.tile([P, HALF], F32, name="abs_frac")
-            nc.scalar.activation(out=abs_frac[:], in_=frac, func=ACT.Abs)
-            nc.scalar.activation(out=trig[:, 0, :], in_=abs_frac[:], func=ACT.Sin, scale=-TWO_PI, bias=math.pi / 2.0)
+            nc.scalar.activation(out=abs_frac[:], in_=tile_frac, func=ACT.Abs)
+            nc.scalar.activation(
+                out=trig_of[j][:, 0, :], in_=abs_frac[:], func=ACT.Sin, scale=-TWO_PI, bias=math.pi / 2.0
+            )
 
-        def project(j):
-            keys_of[j] = []
-            for h in range(2):
-                bank = key_banks.tile([P, HALF], F32, name="key_bank_%d" % h)
-                for g in range(PASSES):
-                    nc.tensor.matmul_mx(
-                        out=bank[:],
-                        lhsT=x_codes[:, j, g * P : (g + 1) * P].bitcast(FP8X4),
-                        lhsT_scale=x_scales[:, j, g * P : (g + 1) * P],
-                        rhs=w_codes[:, h, g * HALF : (g + 1) * HALF].bitcast(FP8X4),
-                        rhs_scale=w_scales[:, h, g * HALF : (g + 1) * HALF],
-                        start=(g == 0),
-                        stop=(g == PASSES - 1),
-                    )
-                keys_of[j].append(bank)
-
-        def rotate(j):
-            trig = trig_of[j // 2][:, j % 2]
-            products = double.tile([P, 2, 2, 2, PAIRS], F32, name="products")
-            for h in range(2):
-                planes = keys_of[j][h][:].rearrange("p (e i) -> p e i", e=2)
-                nc.vector.tensor_mul(
-                    out=products[:, h],
-                    in0=planes.unsqueeze(1).to_broadcast([P, 2, 2, PAIRS]),
-                    in1=trig[:, :, h * PAIRS : (h + 1) * PAIRS].unsqueeze(2).to_broadcast([P, 2, 2, PAIRS]),
+        def project(j, h):
+            bank = key_banks.tile([P, HALF], F32, name="key_bank_%d" % h)
+            for g in range(PASSES):
+                nc.tensor.matmul_mx(
+                    out=bank[:],
+                    lhsT=x_codes[:, j, g * P : (g + 1) * P].bitcast(FP8X4),
+                    lhsT_scale=x_scales[:, j, g * P : (g + 1) * P],
+                    rhs=w_codes[:, h, g * HALF : (g + 1) * HALF].bitcast(FP8X4),
+                    rhs_scale=w_scales[:, h, g * HALF : (g + 1) * HALF],
+                    start=(g == 0),
+                    stop=(g == PASSES - 1),
                 )
-            rotated = triple.tile([P, 2, 2, PAIRS], F32, name="rotated")
-            sums = stats.tile([P, 2], F32, name="sums")
+            keys_of[j, h] = bank
+
+        def multiply(j, h):
+            if h == 0:
+                products_of[j] = triple.tile([P, 2, 2, 2, PAIRS], F32, name="work")
+            planes = keys_of[j, h][:].rearrange("p (e i) -> p e i", e=2)
+            nc.vector.tensor_mul(
+                out=products_of[j][:, h],
+                in0=planes.unsqueeze(1).to_broadcast([P, 2, 2, PAIRS]),
+                in1=trig_of[j][:, :, h * PAIRS : (h + 1) * PAIRS].unsqueeze(2).to_broadcast([P, 2, 2, PAIRS]),
+            )
+
+        def add_products(j):
+            products = products_of[j]
+            rotated_of[j] = quad.tile([P, 2, 2, PAIRS], F32, name="rotated")
+            sums_of[j] = stats.tile([P, 2], F32, name="sums")
             nc.vector.scalar_tensor_tensor(
-                out=rotated[:, :, 0, :], in0=products[:, :, 0, 0, :], scalar=1.0, in1=products[:, :, 1, 1, :],
-                op0=ALU.mult, op1=ALU.subtract, accum_out=sums[:, 0:1],
+                out=rotated_of[j][:, :, 0, :], in0=products[:, :, 0, 0, :], scalar=1.0, in1=products[:, :, 1, 1, :],
+                op0=ALU.mult, op1=ALU.subtract, accum_out=sums_of[j][:, 0:1],
             )
             nc.vector.scalar_tensor_tensor(
-                out=rotated[:, :, 1, :], in0=products[:, :, 0, 1, :], scalar=1.0, in1=products[:, :, 1, 0, :],
-                op0=ALU.mult, op1=ALU.add, accum_out=sums[:, 1:2],
+                out=rotated_of[j][:, :, 1, :], in0=products[:, :, 0, 1, :], scalar=1.0, in1=products[:, :, 1, 0, :],
+                op0=ALU.mult, op1=ALU.add, accum_out=sums_of[j][:, 1:2],
             )
-            minus_mean = stats.tile([P, 1], F32, name="minus_mean")
-            nc.vector.tensor_scalar(
-                out=minus_mean[:], in0=sums[:, 0:1], scalar1=sums[:, 1:2], scalar2=-1.0 / CHANNELS,
-                op0=ALU.add, op1=ALU.mult,
+
+        def negative_mean(j):
+            scaled = stats.tile([P, 2], F32, name="scaled")
+            minus_mean_of[j] = stats.tile([P, 1], F32, name="minus_mean")
+            nc.scalar.activation(
+                out=scaled[:], in_=sums_of[j][:], func=ACT.Copy, scale=-1.0 / CHANNELS, accum_out=minus_mean_of[j][:]
             )
-            rotated_of[j], minus_mean_of[j] = rotated, minus_mean
 
         def sum_of_squares(j):
             squares = double.tile([P, CHANNELS], F32, name="squares")
@@ -214,52 +224,102 @@ def tile_attentionalsplatting_pa_kernel(tc, updated_track_tokens, tracks, W_k, k
             nc.gpsimd.tensor_tensor(out=shift_of[j][:], in0=minus_mean_of[j][:], in1=rstd_of[j][:], op=ALU.mult)
 
         def normalise(j):
-            normed_of[j] = double.tile([P, CHANNELS], F32, name="normed")
+            normed_of[j] = triple.tile([P, CHANNELS], F32, name="normed")
             nc.scalar.activation(
                 out=normed_of[j][:].rearrange("p (h i e) -> p h i e", h=2, e=2),
                 in_=rotated_of[j][:].rearrange("p h e i -> p h i e"),
                 func=ACT.Identity, bias=shift_of[j][:], scale=rstd_of[j][:],
             )
 
-        def apply_gamma_and_store(j):
-            engine = nc.vector if j == TILES - 1 else nc.gpsimd
-            result = triple.tile([P, CHANNELS], F32, name="result")
+        def apply_gamma_and_store(j, engine):
+            result = triple.tile([P, CHANNELS], F32, name="work")
             engine.tensor_tensor(out=result[:], in0=normed_of[j][:], in1=gamma[:], op=ALU.mult)
             nc.sync.dma_start(out=out_dram[:, j, :], in_=result[:])
 
-        angles_in_turns(nc.vector, 0)
-        for pair in range(1, TILES // 2):
-            angles_in_turns(nc.gpsimd, pair)
-        reduce_angles(0)
-        for q in range(W_BLOCKS):
-            flip_weights(q)
-            if q % 2 == 1:
-                quantise_weights(q // 2)
-        flip_tokens(0)
-        cos_and_sin(0)
-        flip_tokens(1)
-        quantise_tokens(0)
-        project(0)
-        reduce_angles(1)
-        cos_and_sin(1)
-        nc.gpsimd.tensor_scalar(out=gamma[:], in0=gamma_bf[:], scalar1=1.0, scalar2=0.0, op0=ALU.mult, op1=ALU.add)
+        def finish_last_tile(j):
+            planes = rotated_of[j][:].rearrange("p h e i -> p h (e i)")
+            centred = [keep.tile([P, HALF], F32, name="centred_%d" % h) for h in range(2)]
+            spare = [keep.tile([P, HALF], F32, name="spare_%d" % h) for h in range(2)]
+            partial = [stats.tile([P, 1], F32, name="partial_%d" % h) for h in range(2)]
+            for h in range(2):
+                nc.vector.tensor_scalar(
+                    out=centred[h][:], in0=planes[:, h], scalar1=minus_mean_of[j][:], scalar2=0.0,
+                    op0=ALU.add, op1=ALU.add,
+                )
+            nc.scalar.activation(
+                out=spare[0][:], in_=centred[0][:], func=ACT.Square, scale=1.0 / ROOT_CHANNELS, accum_out=partial[0][:]
+            )
+            nc.vector.scalar_tensor_tensor(
+                out=spare[1][:], in0=centred[1][:], scalar=1.0 / CHANNELS, in1=centred[1][:],
+                op0=ALU.mult, op1=ALU.mult, accum_out=partial[1][:],
+            )
+            apply_gamma_and_store(j - 1, nc.vector)
+            var_eps = stats.tile([P, 1], F32, name="var_eps")
+            nc.gpsimd.tensor_scalar(
+                out=var_eps[:], in0=partial[0][:], scalar1=partial[1][:], scalar2=EPS, op0=ALU.add, op1=ALU.add
+            )
+            rstd = stats.tile([P, 1], F32, name="rstd")
+            nc.gpsimd.tensor_tensor(out=rstd[:], in0=var_eps[:], in1=minus_half[:], op=ALU.pow)
+            for h in range(2):
+                result = double.tile([P, HALF], F32, name="last_result")
+                nc.vector.scalar_tensor_tensor(
+                    out=result[:].rearrange("p (i e) -> p i e", e=2),
+                    in0=centred[h][:].rearrange("p (e i) -> p i e", e=2),
+                    scalar=rstd[:],
+                    in1=gamma[:, h * HALF : (h + 1) * HALF].rearrange("p (i e) -> p i e", e=2),
+                    op0=ALU.mult, op1=ALU.mult,
+                )
+                nc.sync.dma_start(out=out_dram[:, j, h * HALF : (h + 1) * HALF], in_=result[:])
 
-        for s in range(TILES + 2):
-            if s + 2 < TILES:
-                flip_tokens(s + 2)
+        for j in range(TILES):
+            whole_turns(j)
+        nc.gpsimd.tensor_scalar(out=gamma[:], in0=gamma_bf[:], scalar1=1.0, scalar2=0.0, op0=ALU.mult, op1=ALU.add)
+        reduce_angles(0)
+        flip_weights(0)
+        reduce_angles(1)
+        flip_weights(1)
+        flip_tokens(0, "scalar")
+        quantise_weights(0)
+        cos_and_sin(0)
+        quantise_tokens(0)
+        flip_weights(2)
+        flip_weights(3)
+        flip_tokens(1, "scalar")
+        project(0, 0)
+        quantise_weights(1)
+        multiply(0, 0)
+        project(0, 1)
+        cos_and_sin(1)
+        quantise_tokens(1)
+        flip_tokens(2, "scalar")
+        reduce_angles(2)
+        reduce_angles(3)
+
+        for s in range(TILES):
+            if s + 3 < TILES:
+                flip_tokens(s + 3, "scalar" if s % 2 == 0 else "vector")
             if s + 1 < TILES:
-                quantise_tokens(s + 1)
-                project(s + 1)
-            if 1 <= s <= TILES:
+                project(s + 1, 0)
+                project(s + 1, 1)
+            if s >= 1:
+                negative_mean(s - 1)
+                sum_of_squares(s - 1)
+            if s > 0:
+                multiply(s, 0)
+            multiply(s, 1)
+            if s in GAMMA_ON_GPSIMD:
+                apply_gamma_and_store(GAMMA_ON_GPSIMD[s], nc.gpsimd)
+            if s in GAMMA_ON_VECTOR:
+                apply_gamma_and_store(GAMMA_ON_VECTOR[s], nc.vector)
+            if s >= 1:
                 scale_and_shift(s - 1)
             if s + 2 < TILES:
+                quantise_tokens(s + 2)
                 cos_and_sin(s + 2)
-            if 1 <= s <= TILES:
+            if s + 4 < TILES:
+                reduce_angles(s + 4)
+            add_products(s)
+            if s >= 1:
                 normalise(s - 1)
-            if s >= 2:
-                apply_gamma_and_store(s - 2)
-            if s < TILES:
-                rotate(s)
-                if s % 2 == 1 and s + 3 < TILES:
-                    reduce_angles((s + 3) // 2)
-                sum_of_squares(s)
+        negative_mean(TILES - 1)
+        finish_last_tile(TILES - 1)

@@ -90,7 +90,6 @@ def tile_attentionalsplatting_pa_kernel(tc, updated_track_tokens, tracks, W_k, k
         pos = keep.tile([P, 2 * TILES], F32)
         nc.vector.tensor_copy(out=pos[:], in_=pos_bf[:])
         gamma = keep.tile([P, CHANNELS], F32)
-        whole = keep.tile([P, 2 * TILES, PAIRS], I32)
         frac = keep.tile([P, 2 * TILES, PAIRS], F32)
 
         w_grouped = keep.tile([P, 2, PASSES * HALF * 4], BF16, align_bytes=64)
@@ -136,26 +135,24 @@ def tile_attentionalsplatting_pa_kernel(tc, updated_track_tokens, tracks, W_k, k
                 out=x_codes[:, j, :].bitcast(FP8X4), scales=x_scales[:, j, :], in_=x_grouped[:, j, :]
             )
 
-        def whole_turns(j):
-            for column in (2 * j, 2 * j + 1):
-                nc.gpsimd.tensor_scalar(
-                    out=whole[:, column, :], in0=theta[:], scalar1=pos[:, column : column + 1], scalar2=0.0,
-                    op0=ALU.mult, op1=ALU.add,
-                )
-
         def reduce_angles(j):
-            for column in (2 * j, 2 * j + 1):
+            whole = double.tile([P, 2, PAIRS], I32, name="whole")
+            for h in range(2):
+                nc.vector.tensor_scalar_mul(
+                    out=whole[:, h, :], in0=theta[:], scalar1=pos[:, 2 * j + h : 2 * j + h + 1]
+                )
+            for h in range(2):
                 nc.vector.scalar_tensor_tensor(
-                    out=frac[:, column, :], in0=theta[:], scalar=pos[:, column : column + 1],
-                    in1=whole[:, column, :], op0=ALU.mult, op1=ALU.subtract,
+                    out=frac[:, 2 * j + h, :], in0=theta[:], scalar=pos[:, 2 * j + h : 2 * j + h + 1],
+                    in1=whole[:, h, :], op0=ALU.mult, op1=ALU.subtract,
                 )
 
         def cos_and_sin(j):
             tile_frac = frac[:, 2 * j : 2 * j + 2, :].rearrange("p h i -> p (h i)")
             trig_of[j] = quad.tile([P, 2, HALF], F32, name="trig")
-            nc.scalar.activation(out=trig_of[j][:, 1, :], in_=tile_frac, func=ACT.Sin, scale=TWO_PI)
             abs_frac = double.tile([P, HALF], F32, name="abs_frac")
             nc.scalar.activation(out=abs_frac[:], in_=tile_frac, func=ACT.Abs)
+            nc.scalar.activation(out=trig_of[j][:, 1, :], in_=tile_frac, func=ACT.Sin, scale=TWO_PI)
             nc.scalar.activation(
                 out=trig_of[j][:, 0, :], in_=abs_frac[:], func=ACT.Sin, scale=-TWO_PI, bias=math.pi / 2.0
             )
@@ -271,8 +268,6 @@ def tile_attentionalsplatting_pa_kernel(tc, updated_track_tokens, tracks, W_k, k
                 )
                 nc.sync.dma_start(out=out_dram[:, j, h * HALF : (h + 1) * HALF], in_=result[:])
 
-        for j in range(TILES):
-            whole_turns(j)
         nc.gpsimd.tensor_scalar(out=gamma[:], in0=gamma_bf[:], scalar1=1.0, scalar2=0.0, op0=ALU.mult, op1=ALU.add)
         reduce_angles(0)
         flip_weights(0)
@@ -280,30 +275,26 @@ def tile_attentionalsplatting_pa_kernel(tc, updated_track_tokens, tracks, W_k, k
         flip_weights(1)
         flip_tokens(0, "scalar")
         quantise_weights(0)
-        cos_and_sin(0)
         quantise_tokens(0)
+        cos_and_sin(0)
         flip_weights(2)
+        reduce_angles(2)
         flip_weights(3)
         flip_tokens(1, "scalar")
         project(0, 0)
         quantise_weights(1)
         multiply(0, 0)
         project(0, 1)
-        cos_and_sin(1)
         quantise_tokens(1)
+        cos_and_sin(1)
         flip_tokens(2, "scalar")
-        reduce_angles(2)
-        reduce_angles(3)
 
         for s in range(TILES):
             if s + 3 < TILES:
-                flip_tokens(s + 3, "scalar" if s % 2 == 0 else "vector")
+                flip_tokens(s + 3, "scalar")
             if s + 1 < TILES:
                 project(s + 1, 0)
                 project(s + 1, 1)
-            if s >= 1:
-                negative_mean(s - 1)
-                sum_of_squares(s - 1)
             if s > 0:
                 multiply(s, 0)
             multiply(s, 1)
@@ -312,12 +303,14 @@ def tile_attentionalsplatting_pa_kernel(tc, updated_track_tokens, tracks, W_k, k
             if s in GAMMA_ON_VECTOR:
                 apply_gamma_and_store(GAMMA_ON_VECTOR[s], nc.vector)
             if s >= 1:
+                negative_mean(s - 1)
+                sum_of_squares(s - 1)
                 scale_and_shift(s - 1)
             if s + 2 < TILES:
                 quantise_tokens(s + 2)
                 cos_and_sin(s + 2)
-            if s + 4 < TILES:
-                reduce_angles(s + 4)
+            if s + 3 < TILES:
+                reduce_angles(s + 3)
             add_products(s)
             if s >= 1:
                 normalise(s - 1)

@@ -49,7 +49,7 @@ def tile_attentionalsplatting_pa_kernel(tc, updated_track_tokens, tracks, W_k, k
         double = ctx.enter_context(tc.tile_pool(name="double", bufs=2))
         triple = ctx.enter_context(tc.tile_pool(name="triple", bufs=3))
         quad = ctx.enter_context(tc.tile_pool(name="quad", bufs=4))
-        stats = ctx.enter_context(tc.tile_pool(name="stats", bufs=4))
+        stats = ctx.enter_context(tc.tile_pool(name="stats", bufs=6))
         flip_banks = ctx.enter_context(tc.psum_pool(name="flip_banks", bufs=4))
         key_banks = ctx.enter_context(tc.psum_pool(name="key_banks", bufs=2))
         ctx.enter_context(tc.manual_schedule())
@@ -209,7 +209,7 @@ def tile_attentionalsplatting_pa_kernel(tc, updated_track_tokens, tracks, W_k, k
                 bias=minus_mean_of[j][:], scale=1.0, accum_out=sum_squares_of[j][:],
             )
 
-        def scale_and_shift(j):
+        def scale_from_variance(j):
             var_eps = stats.tile([P, 1], F32, name="var_eps")
             nc.gpsimd.tensor_scalar(
                 out=var_eps[:], in0=sum_squares_of[j][:], scalar1=1.0 / CHANNELS, scalar2=EPS,
@@ -217,8 +217,10 @@ def tile_attentionalsplatting_pa_kernel(tc, updated_track_tokens, tracks, W_k, k
             )
             rstd_of[j] = stats.tile([P, 1], F32, name="rstd")
             nc.gpsimd.tensor_tensor(out=rstd_of[j][:], in0=var_eps[:], in1=minus_half[:], op=ALU.pow)
+
+        def shift_from_scale(j):
             shift_of[j] = stats.tile([P, 1], F32, name="shift")
-            nc.gpsimd.tensor_tensor(out=shift_of[j][:], in0=minus_mean_of[j][:], in1=rstd_of[j][:], op=ALU.mult)
+            nc.scalar.activation(out=shift_of[j][:], in_=minus_mean_of[j][:], func=ACT.Copy, scale=rstd_of[j][:])
 
         def normalise(j):
             normed_of[j] = triple.tile([P, CHANNELS], F32, name="normed")
@@ -298,21 +300,26 @@ def tile_attentionalsplatting_pa_kernel(tc, updated_track_tokens, tracks, W_k, k
             if s > 0:
                 multiply(s, 0)
             multiply(s, 1)
+            if s >= 2:
+                shift_from_scale(s - 2)
+            if s >= 1:
+                negative_mean(s - 1)
+            if s >= 2:
+                normalise(s - 2)
             if s in GAMMA_ON_GPSIMD:
                 apply_gamma_and_store(GAMMA_ON_GPSIMD[s], nc.gpsimd)
             if s in GAMMA_ON_VECTOR:
                 apply_gamma_and_store(GAMMA_ON_VECTOR[s], nc.vector)
             if s >= 1:
-                negative_mean(s - 1)
                 sum_of_squares(s - 1)
-                scale_and_shift(s - 1)
+                scale_from_variance(s - 1)
             if s + 2 < TILES:
                 quantise_tokens(s + 2)
                 cos_and_sin(s + 2)
             if s + 3 < TILES:
                 reduce_angles(s + 3)
             add_products(s)
-            if s >= 1:
-                normalise(s - 1)
+        shift_from_scale(TILES - 2)
+        normalise(TILES - 2)
         negative_mean(TILES - 1)
         finish_last_tile(TILES - 1)

@@ -30,8 +30,6 @@ EPS = 1e-6
 THETA_BASE = 100.0
 TWO_PI = 2.0 * math.pi
 ROOT_CHANNELS = math.sqrt(CHANNELS)
-GAMMA_ON_GPSIMD = {3: 0, 4: 1, 5: 2, 6: 3}
-GAMMA_ON_VECTOR = {6: 4, 7: 5}
 
 FLOPS = 2 * TOKENS * D * CHANNELS
 
@@ -102,33 +100,30 @@ def tile_attentionalsplatting_pa_kernel(tc, updated_track_tokens, tracks, W_k, k
         trig_of, keys_of, products_of, rotated_of, sums_of, minus_mean_of = {}, {}, {}, {}, {}, {}
         sum_squares_of, rstd_of, shift_of, normed_of = {}, {}, {}, {}
 
-        def flip_rows(words, grouped_words, copy_engine):
+        def flip_rows(words, grouped_words):
             bank = flip_banks.tile([P, PASSES * 2 * P], F32, name="flip_bank")
             for t in range(PASSES * 2):
                 g, u = divmod(t, 2)
                 every_second = words[:, g * 2 * P + u : (g + 1) * 2 * P : 2]
                 nc.tensor.transpose(bank[:, t * P : (t + 1) * P], every_second, ident[:])
             planes = bank[:].rearrange("p (g u r) -> p g r u", g=PASSES, u=2)
-            if copy_engine == "scalar":
-                nc.scalar.copy(out=grouped_words, in_=planes)
-            else:
-                nc.vector.tensor_copy(out=grouped_words, in_=planes)
+            nc.scalar.copy(out=grouped_words, in_=planes)
 
         def flip_weights(q):
             h, b = divmod(q, W_BLOCKS // 2)
             half_words = w_grouped[:, h, :].bitcast(F32).rearrange("p (g c u) -> p g c u", g=PASSES, u=2)
-            for e, copy_engine in enumerate(["scalar", "vector"]):
+            for e in range(2):
                 first = e * PAIRS + b * P
-                flip_rows(w_raw[:, q, e, :].bitcast(F32), half_words[:, :, first : first + P, :], copy_engine)
+                flip_rows(w_raw[:, q, e, :].bitcast(F32), half_words[:, :, first : first + P, :])
 
         def quantise_weights(h):
             nc.vector.quantize_mx(
                 out=w_codes[:, h, :].bitcast(FP8X4), scales=w_scales[:, h, :], in_=w_grouped[:, h, :]
             )
 
-        def flip_tokens(j, copy_engine):
+        def flip_tokens(j):
             tile_words = x_grouped[:, j, :].bitcast(F32).rearrange("p (g r u) -> p g r u", g=PASSES, u=2)
-            flip_rows(x_raw[:, j, :].bitcast(F32), tile_words, copy_engine)
+            flip_rows(x_raw[:, j, :].bitcast(F32), tile_words)
 
         def quantise_tokens(j):
             nc.vector.quantize_mx(
@@ -173,7 +168,7 @@ def tile_attentionalsplatting_pa_kernel(tc, updated_track_tokens, tracks, W_k, k
 
         def multiply(j, h):
             if h == 0:
-                products_of[j] = triple.tile([P, 2, 2, 2, PAIRS], F32, name="work")
+                products_of[j] = double.tile([P, 2, 2, 2, PAIRS], F32, name="products")
             planes = keys_of[j, h][:].rearrange("p (e i) -> p e i", e=2)
             nc.vector.tensor_mul(
                 out=products_of[j][:, h],
@@ -230,9 +225,9 @@ def tile_attentionalsplatting_pa_kernel(tc, updated_track_tokens, tracks, W_k, k
                 func=ACT.Identity, bias=shift_of[j][:], scale=rstd_of[j][:],
             )
 
-        def apply_gamma_and_store(j, engine):
-            result = triple.tile([P, CHANNELS], F32, name="work")
-            engine.tensor_tensor(out=result[:], in0=normed_of[j][:], in1=gamma[:], op=ALU.mult)
+        def apply_gamma_and_store(j):
+            result = quad.tile([P, CHANNELS], F32, name="result")
+            nc.vector.tensor_tensor(out=result[:], in0=normed_of[j][:], in1=gamma[:], op=ALU.mult)
             nc.sync.dma_start(out=out_dram[:, j, :], in_=result[:])
 
         def finish_last_tile(j):
@@ -252,7 +247,9 @@ def tile_attentionalsplatting_pa_kernel(tc, updated_track_tokens, tracks, W_k, k
                 out=spare[1][:], in0=centred[1][:], scalar=1.0 / CHANNELS, in1=centred[1][:],
                 op0=ALU.mult, op1=ALU.mult, accum_out=partial[1][:],
             )
-            apply_gamma_and_store(j - 1, nc.vector)
+            shift_from_scale(j - 1)
+            normalise(j - 1)
+            apply_gamma_and_store(j - 1)
             var_eps = stats.tile([P, 1], F32, name="var_eps")
             nc.gpsimd.tensor_scalar(
                 out=var_eps[:], in0=partial[0][:], scalar1=partial[1][:], scalar2=EPS, op0=ALU.add, op1=ALU.add
@@ -272,28 +269,32 @@ def tile_attentionalsplatting_pa_kernel(tc, updated_track_tokens, tracks, W_k, k
 
         nc.gpsimd.tensor_scalar(out=gamma[:], in0=gamma_bf[:], scalar1=1.0, scalar2=0.0, op0=ALU.mult, op1=ALU.add)
         reduce_angles(0)
-        flip_weights(0)
         reduce_angles(1)
+        cos_and_sin(0)
+        flip_weights(0)
+        reduce_angles(2)
+        reduce_angles(3)
+        reduce_angles(4)
         flip_weights(1)
-        flip_tokens(0, "scalar")
+        flip_tokens(0)
         quantise_weights(0)
         quantise_tokens(0)
-        cos_and_sin(0)
         flip_weights(2)
-        reduce_angles(2)
+        reduce_angles(5)
+        reduce_angles(6)
         flip_weights(3)
-        flip_tokens(1, "scalar")
+        flip_tokens(1)
         project(0, 0)
         quantise_weights(1)
         multiply(0, 0)
         project(0, 1)
         quantise_tokens(1)
         cos_and_sin(1)
-        flip_tokens(2, "scalar")
+        flip_tokens(2)
 
         for s in range(TILES):
             if s + 3 < TILES:
-                flip_tokens(s + 3, "scalar")
+                flip_tokens(s + 3)
             if s + 1 < TILES:
                 project(s + 1, 0)
                 project(s + 1, 1)
@@ -306,20 +307,16 @@ def tile_attentionalsplatting_pa_kernel(tc, updated_track_tokens, tracks, W_k, k
                 negative_mean(s - 1)
             if s >= 2:
                 normalise(s - 2)
-            if s in GAMMA_ON_GPSIMD:
-                apply_gamma_and_store(GAMMA_ON_GPSIMD[s], nc.gpsimd)
-            if s in GAMMA_ON_VECTOR:
-                apply_gamma_and_store(GAMMA_ON_VECTOR[s], nc.vector)
+            if s >= 2:
+                apply_gamma_and_store(s - 2)
             if s >= 1:
                 sum_of_squares(s - 1)
                 scale_from_variance(s - 1)
             if s + 2 < TILES:
                 quantise_tokens(s + 2)
                 cos_and_sin(s + 2)
-            if s + 3 < TILES:
-                reduce_angles(s + 3)
+            if s == 0:
+                reduce_angles(7)
             add_products(s)
-        shift_from_scale(TILES - 2)
-        normalise(TILES - 2)
         negative_mean(TILES - 1)
         finish_last_tile(TILES - 1)

@@ -30,6 +30,8 @@ EPS = 1e-6
 THETA_BASE = 100.0
 TWO_PI = 2.0 * math.pi
 ROOT_CHANNELS = math.sqrt(CHANNELS)
+GAMMA_ON_GPSIMD = 4
+FIRST_COPIED_BY_VECTOR = 6
 
 FLOPS = 2 * TOKENS * D * CHANNELS
 
@@ -100,14 +102,17 @@ def tile_attentionalsplatting_pa_kernel(tc, updated_track_tokens, tracks, W_k, k
         trig_of, keys_of, products_of, rotated_of, sums_of, minus_mean_of = {}, {}, {}, {}, {}, {}
         sum_squares_of, rstd_of, shift_of, normed_of = {}, {}, {}, {}
 
-        def flip_rows(words, grouped_words):
+        def flip_rows(words, grouped_words, copy_engine="scalar"):
             bank = flip_banks.tile([P, PASSES * 2 * P], F32, name="flip_bank")
             for t in range(PASSES * 2):
                 g, u = divmod(t, 2)
                 every_second = words[:, g * 2 * P + u : (g + 1) * 2 * P : 2]
                 nc.tensor.transpose(bank[:, t * P : (t + 1) * P], every_second, ident[:])
             planes = bank[:].rearrange("p (g u r) -> p g r u", g=PASSES, u=2)
-            nc.scalar.copy(out=grouped_words, in_=planes)
+            if copy_engine == "scalar":
+                nc.scalar.copy(out=grouped_words, in_=planes)
+            else:
+                nc.vector.tensor_copy(out=grouped_words, in_=planes)
 
         def flip_weights(q):
             h, b = divmod(q, W_BLOCKS // 2)
@@ -121,9 +126,9 @@ def tile_attentionalsplatting_pa_kernel(tc, updated_track_tokens, tracks, W_k, k
                 out=w_codes[:, h, :].bitcast(FP8X4), scales=w_scales[:, h, :], in_=w_grouped[:, h, :]
             )
 
-        def flip_tokens(j):
+        def flip_tokens(j, copy_engine="scalar"):
             tile_words = x_grouped[:, j, :].bitcast(F32).rearrange("p (g r u) -> p g r u", g=PASSES, u=2)
-            flip_rows(x_raw[:, j, :].bitcast(F32), tile_words)
+            flip_rows(x_raw[:, j, :].bitcast(F32), tile_words, copy_engine)
 
         def quantise_tokens(j):
             nc.vector.quantize_mx(
@@ -168,7 +173,7 @@ def tile_attentionalsplatting_pa_kernel(tc, updated_track_tokens, tracks, W_k, k
 
         def multiply(j, h):
             if h == 0:
-                products_of[j] = double.tile([P, 2, 2, 2, PAIRS], F32, name="products")
+                products_of[j] = triple.tile([P, 2, 2, 2, PAIRS], F32, name="work")
             planes = keys_of[j, h][:].rearrange("p (e i) -> p e i", e=2)
             nc.vector.tensor_mul(
                 out=products_of[j][:, h],
@@ -225,9 +230,12 @@ def tile_attentionalsplatting_pa_kernel(tc, updated_track_tokens, tracks, W_k, k
                 func=ACT.Identity, bias=shift_of[j][:], scale=rstd_of[j][:],
             )
 
-        def apply_gamma_and_store(j):
-            result = quad.tile([P, CHANNELS], F32, name="result")
-            nc.vector.tensor_tensor(out=result[:], in0=normed_of[j][:], in1=gamma[:], op=ALU.mult)
+        def apply_gamma_and_store(j, engine):
+            if engine is nc.gpsimd:
+                result = triple.tile([P, CHANNELS], F32, name="work")
+            else:
+                result = triple.tile([P, CHANNELS], F32, name="result")
+            engine.tensor_tensor(out=result[:], in0=normed_of[j][:], in1=gamma[:], op=ALU.mult)
             nc.sync.dma_start(out=out_dram[:, j, :], in_=result[:])
 
         def finish_last_tile(j):
@@ -247,9 +255,10 @@ def tile_attentionalsplatting_pa_kernel(tc, updated_track_tokens, tracks, W_k, k
                 out=spare[1][:], in0=centred[1][:], scalar=1.0 / CHANNELS, in1=centred[1][:],
                 op0=ALU.mult, op1=ALU.mult, accum_out=partial[1][:],
             )
+            apply_gamma_and_store(j - 2, nc.vector)
             shift_from_scale(j - 1)
             normalise(j - 1)
-            apply_gamma_and_store(j - 1)
+            apply_gamma_and_store(j - 1, nc.vector)
             var_eps = stats.tile([P, 1], F32, name="var_eps")
             nc.gpsimd.tensor_scalar(
                 out=var_eps[:], in0=partial[0][:], scalar1=partial[1][:], scalar2=EPS, op0=ALU.add, op1=ALU.add
@@ -293,30 +302,31 @@ def tile_attentionalsplatting_pa_kernel(tc, updated_track_tokens, tracks, W_k, k
         flip_tokens(2)
 
         for s in range(TILES):
+            if s >= 1:
+                negative_mean(s - 1)
             if s + 3 < TILES:
-                flip_tokens(s + 3)
+                flip_tokens(s + 3, "scalar" if s + 3 < FIRST_COPIED_BY_VECTOR else "vector")
             if s + 1 < TILES:
                 project(s + 1, 0)
                 project(s + 1, 1)
             if s > 0:
                 multiply(s, 0)
             multiply(s, 1)
-            if s >= 2:
-                shift_from_scale(s - 2)
-            if s >= 1:
-                negative_mean(s - 1)
-            if s >= 2:
-                normalise(s - 2)
-            if s >= 2:
-                apply_gamma_and_store(s - 2)
+            if 3 <= s < 3 + GAMMA_ON_GPSIMD:
+                apply_gamma_and_store(s - 3, nc.gpsimd)
             if s >= 1:
                 sum_of_squares(s - 1)
                 scale_from_variance(s - 1)
+            if s >= 2:
+                shift_from_scale(s - 2)
+                normalise(s - 2)
             if s + 2 < TILES:
                 quantise_tokens(s + 2)
                 cos_and_sin(s + 2)
             if s == 0:
                 reduce_angles(7)
             add_products(s)
+            if s >= 3 + GAMMA_ON_GPSIMD:
+                apply_gamma_and_store(s - 3, nc.vector)
         negative_mean(TILES - 1)
         finish_last_tile(TILES - 1)

@@ -29,7 +29,6 @@ WORDS = D // 2
 EPS = 1e-6
 THETA_BASE = 100.0
 TWO_PI = 2.0 * math.pi
-ROOT_CHANNELS = math.sqrt(CHANNELS)
 GAMMA_ON_GPSIMD = 4
 FIRST_COPIED_BY_VECTOR = 6
 
@@ -65,7 +64,8 @@ def tile_attentionalsplatting_pa_kernel(tc, updated_track_tokens, tracks, W_k, k
         def load_tokens(j):
             nc.sync.dma_start(out=x_raw[:, j : j + 2, :], in_=x_dram[:, j : j + 2, :])
 
-        load_weights(0)
+        for e in range(2):
+            nc.sync.dma_start(out=w_raw[:, 0, e, :], in_=w_dram[0][:, e * D : (e + 1) * D])
         load_weights(1)
         load_tokens(0)
         load_weights(2)
@@ -79,9 +79,11 @@ def tile_attentionalsplatting_pa_kernel(tc, updated_track_tokens, tracks, W_k, k
         make_identity(nc, ident[:])
         minus_half = keep.tile([P, 1], F32)
         nc.gpsimd.memset(minus_half[:], -0.5)
-        theta = keep.tile([P, PAIRS], F32)
         one = keep.tile([P, 1], F32)
         nc.vector.memset(one[:], 1.0)
+        first_sin = keep.tile([P, 1], F32)
+        nc.scalar.activation(out=first_sin[:], in_=one[:], func=ACT.Sin)
+        theta = keep.tile([P, PAIRS], F32)
         nc.vector.tensor_scalar_mul(out=theta[:, 0:1], in0=one[:], scalar1=1.0 / TWO_PI)
         for w in [2**doubling for doubling in range(DOUBLINGS)]:
             nc.vector.tensor_scalar_mul(
@@ -240,37 +242,24 @@ def tile_attentionalsplatting_pa_kernel(tc, updated_track_tokens, tracks, W_k, k
 
         def finish_last_tile(j):
             planes = rotated_of[j][:].rearrange("p h e i -> p h (e i)")
+            sum_of_squares(j)
+            apply_gamma_and_store(j - 2, nc.vector)
             centred = [keep.tile([P, HALF], F32, name="centred_%d" % h) for h in range(2)]
-            spare = [keep.tile([P, HALF], F32, name="spare_%d" % h) for h in range(2)]
-            partial = [stats.tile([P, 1], F32, name="partial_%d" % h) for h in range(2)]
             for h in range(2):
                 nc.vector.tensor_scalar(
                     out=centred[h][:], in0=planes[:, h], scalar1=minus_mean_of[j][:], scalar2=0.0,
                     op0=ALU.add, op1=ALU.add,
                 )
-            nc.scalar.activation(
-                out=spare[0][:], in_=centred[0][:], func=ACT.Square, scale=1.0 / ROOT_CHANNELS, accum_out=partial[0][:]
-            )
-            nc.vector.scalar_tensor_tensor(
-                out=spare[1][:], in0=centred[1][:], scalar=1.0 / CHANNELS, in1=centred[1][:],
-                op0=ALU.mult, op1=ALU.mult, accum_out=partial[1][:],
-            )
-            apply_gamma_and_store(j - 2, nc.vector)
             shift_from_scale(j - 1)
             normalise(j - 1)
             apply_gamma_and_store(j - 1, nc.vector)
-            var_eps = stats.tile([P, 1], F32, name="var_eps")
-            nc.gpsimd.tensor_scalar(
-                out=var_eps[:], in0=partial[0][:], scalar1=partial[1][:], scalar2=EPS, op0=ALU.add, op1=ALU.add
-            )
-            rstd = stats.tile([P, 1], F32, name="rstd")
-            nc.gpsimd.tensor_tensor(out=rstd[:], in0=var_eps[:], in1=minus_half[:], op=ALU.pow)
+            scale_from_variance(j)
             for h in range(2):
                 result = double.tile([P, HALF], F32, name="last_result")
                 nc.vector.scalar_tensor_tensor(
                     out=result[:].rearrange("p (i e) -> p i e", e=2),
                     in0=centred[h][:].rearrange("p (e i) -> p i e", e=2),
-                    scalar=rstd[:],
+                    scalar=rstd_of[j][:],
                     in1=gamma[:, h * HALF : (h + 1) * HALF].rearrange("p (i e) -> p i e", e=2),
                     op0=ALU.mult, op1=ALU.mult,
                 )

@@ -29,6 +29,7 @@ WORDS = D // 2
 EPS = 1e-6
 THETA_BASE = 100.0
 TWO_PI = 2.0 * math.pi
+GPSIMD_COLUMNS = 768
 GAMMA_ON_GPSIMD = 4
 FIRST_COPIED_BY_VECTOR = 6
 
@@ -232,18 +233,24 @@ def tile_attentionalsplatting_pa_kernel(tc, updated_track_tokens, tracks, W_k, k
                 func=ACT.Identity, bias=shift_of[j][:], scale=rstd_of[j][:],
             )
 
-        def apply_gamma_and_store(j, engine):
-            if engine is nc.gpsimd:
+        def apply_gamma_and_store(j, shared):
+            if shared:
                 result = triple.tile([P, CHANNELS], F32, name="work")
+                nc.gpsimd.tensor_tensor(
+                    out=result[:, 0:GPSIMD_COLUMNS], in0=normed_of[j][:, 0:GPSIMD_COLUMNS], in1=gamma[:, 0:GPSIMD_COLUMNS], op=ALU.mult
+                )
+                nc.vector.tensor_tensor(
+                    out=result[:, GPSIMD_COLUMNS:], in0=normed_of[j][:, GPSIMD_COLUMNS:], in1=gamma[:, GPSIMD_COLUMNS:], op=ALU.mult
+                )
             else:
                 result = triple.tile([P, CHANNELS], F32, name="result")
-            engine.tensor_tensor(out=result[:], in0=normed_of[j][:], in1=gamma[:], op=ALU.mult)
+                nc.vector.tensor_tensor(out=result[:], in0=normed_of[j][:], in1=gamma[:], op=ALU.mult)
             nc.sync.dma_start(out=out_dram[:, j, :], in_=result[:])
 
         def finish_last_tile(j):
             planes = rotated_of[j][:].rearrange("p h e i -> p h (e i)")
             sum_of_squares(j)
-            apply_gamma_and_store(j - 2, nc.vector)
+            apply_gamma_and_store(j - 2, False)
             centred = [keep.tile([P, HALF], F32, name="centred_%d" % h) for h in range(2)]
             for h in range(2):
                 nc.vector.tensor_scalar(
@@ -252,7 +259,7 @@ def tile_attentionalsplatting_pa_kernel(tc, updated_track_tokens, tracks, W_k, k
                 )
             shift_from_scale(j - 1)
             normalise(j - 1)
-            apply_gamma_and_store(j - 1, nc.vector)
+            apply_gamma_and_store(j - 1, False)
             scale_from_variance(j)
             for h in range(2):
                 result = double.tile([P, HALF], F32, name="last_result")
@@ -301,21 +308,22 @@ def tile_attentionalsplatting_pa_kernel(tc, updated_track_tokens, tracks, W_k, k
             if s > 0:
                 multiply(s, 0)
             multiply(s, 1)
-            if 3 <= s < 3 + GAMMA_ON_GPSIMD:
-                apply_gamma_and_store(s - 3, nc.gpsimd)
             if s >= 1:
                 sum_of_squares(s - 1)
-                scale_from_variance(s - 1)
             if s >= 2:
                 shift_from_scale(s - 2)
                 normalise(s - 2)
             if s + 2 < TILES:
                 quantise_tokens(s + 2)
                 cos_and_sin(s + 2)
+            if 3 <= s < 3 + GAMMA_ON_GPSIMD:
+                apply_gamma_and_store(s - 3, True)
+            if s >= 1:
+                scale_from_variance(s - 1)
             if s == 0:
                 reduce_angles(7)
             add_products(s)
             if s >= 3 + GAMMA_ON_GPSIMD:
-                apply_gamma_and_store(s - 3, nc.vector)
+                apply_gamma_and_store(s - 3, False)
         negative_mean(TILES - 1)
         finish_last_tile(TILES - 1)

@@ -73,8 +73,8 @@ def tile_attentionalsplatting_pa_kernel(tc, updated_track_tokens, tracks, W_k, k
         load_weights(3)
         for j in range(2, TILES, 2):
             load_tokens(j)
-        gamma_bf = keep.tile([P, CHANNELS], BF16)
-        nc.sync.dma_start(out=gamma_bf[:], in_=k_gamma.partition_broadcast(P))
+        gamma = keep.tile([P, CHANNELS], BF16)
+        nc.sync.dma_start(out=gamma[:], in_=k_gamma.partition_broadcast(P))
 
         ident = keep.tile([P, P], F32)
         make_identity(nc, ident[:])
@@ -92,7 +92,6 @@ def tile_attentionalsplatting_pa_kernel(tc, updated_track_tokens, tracks, W_k, k
             )
         pos = keep.tile([P, 2 * TILES], F32)
         nc.vector.tensor_copy(out=pos[:], in_=pos_bf[:])
-        gamma = keep.tile([P, CHANNELS], F32)
         frac = keep.tile([P, 2 * TILES, PAIRS], F32)
 
         w_grouped = keep.tile([P, 2, PASSES * HALF * 4], BF16, align_bytes=64)
@@ -103,7 +102,7 @@ def tile_attentionalsplatting_pa_kernel(tc, updated_track_tokens, tracks, W_k, k
         x_scales = keep.tile([P, TILES, PASSES * P], U8, align_bytes=64)
 
         trig_of, keys_of, products_of, rotated_of, sums_of, minus_mean_of = {}, {}, {}, {}, {}, {}
-        sum_squares_of, rstd_of, shift_of, normed_of = {}, {}, {}, {}
+        sum_squares_of, rstd_of, shift_of, normed_of, weighted_of = {}, {}, {}, {}, {}
 
         def flip_rows(words, grouped_words, copy_engine="scalar"):
             bank = flip_banks.tile([P, PASSES * 2 * P], F32, name="flip_bank")
@@ -247,32 +246,30 @@ def tile_attentionalsplatting_pa_kernel(tc, updated_track_tokens, tracks, W_k, k
                 nc.vector.tensor_tensor(out=result[:], in0=normed_of[j][:], in1=gamma[:], op=ALU.mult)
             nc.sync.dma_start(out=out_dram[:, j, :], in_=result[:])
 
-        def finish_last_tile(j):
-            planes = rotated_of[j][:].rearrange("p h e i -> p h (e i)")
-            sum_of_squares(j)
-            apply_gamma_and_store(j - 2, False)
-            centred = [keep.tile([P, HALF], F32, name="centred_%d" % h) for h in range(2)]
+        def centre_and_apply_gamma(j):
+            weighted_of[j] = keep.tile([P, CHANNELS], F32, name="weighted_%d" % j)
             for h in range(2):
-                nc.vector.tensor_scalar(
-                    out=centred[h][:], in0=planes[:, h], scalar1=minus_mean_of[j][:], scalar2=0.0,
-                    op0=ALU.add, op1=ALU.add,
-                )
-            shift_from_scale(j - 1)
-            normalise(j - 1)
-            apply_gamma_and_store(j - 1, False)
-            scale_from_variance(j)
-            for h in range(2):
-                result = double.tile([P, HALF], F32, name="last_result")
+                columns = slice(h * HALF, (h + 1) * HALF)
                 nc.vector.scalar_tensor_tensor(
-                    out=result[:].rearrange("p (i e) -> p i e", e=2),
-                    in0=centred[h][:].rearrange("p (e i) -> p i e", e=2),
-                    scalar=rstd_of[j][:],
-                    in1=gamma[:, h * HALF : (h + 1) * HALF].rearrange("p (i e) -> p i e", e=2),
-                    op0=ALU.mult, op1=ALU.mult,
+                    out=weighted_of[j][:, columns].rearrange("p (i e) -> p i e", e=2),
+                    in0=rotated_of[j][:, h].rearrange("p e i -> p i e"),
+                    scalar=minus_mean_of[j][:],
+                    in1=gamma[:, columns].rearrange("p (i e) -> p i e", e=2),
+                    op0=ALU.add, op1=ALU.mult,
                 )
-                nc.sync.dma_start(out=out_dram[:, j, h * HALF : (h + 1) * HALF], in_=result[:])
 
-        nc.gpsimd.tensor_scalar(out=gamma[:], in0=gamma_bf[:], scalar1=1.0, scalar2=0.0, op0=ALU.mult, op1=ALU.add)
+        def scale_and_store(j, engine):
+            for h in range(2):
+                columns = slice(h * HALF, (h + 1) * HALF)
+                result = quad.tile([P, HALF], F32, name="half_result")
+                if engine is nc.scalar:
+                    nc.scalar.activation(
+                        out=result[:], in_=weighted_of[j][:, columns], func=ACT.Copy, scale=rstd_of[j][:]
+                    )
+                else:
+                    nc.vector.tensor_scalar_mul(out=result[:], in0=weighted_of[j][:, columns], scalar1=rstd_of[j][:])
+                nc.sync.dma_start(out=out_dram[:, j, columns], in_=result[:])
+
         reduce_angles(0)
         reduce_angles(1)
         cos_and_sin(0)
@@ -280,22 +277,23 @@ def tile_attentionalsplatting_pa_kernel(tc, updated_track_tokens, tracks, W_k, k
         reduce_angles(2)
         reduce_angles(3)
         reduce_angles(4)
+        reduce_angles(5)
         flip_weights(1)
         flip_tokens(0)
         quantise_weights(0)
         quantise_tokens(0)
         flip_weights(2)
-        reduce_angles(5)
         reduce_angles(6)
+        reduce_angles(7)
         flip_weights(3)
         flip_tokens(1)
         project(0, 0)
         quantise_weights(1)
         multiply(0, 0)
-        project(0, 1)
-        quantise_tokens(1)
         cos_and_sin(1)
         flip_tokens(2)
+        project(0, 1)
+        quantise_tokens(1)
 
         for s in range(TILES):
             if s >= 1:
@@ -320,10 +318,14 @@ def tile_attentionalsplatting_pa_kernel(tc, updated_track_tokens, tracks, W_k, k
                 apply_gamma_and_store(s - 3, True)
             if s >= 1:
                 scale_from_variance(s - 1)
-            if s == 0:
-                reduce_angles(7)
             add_products(s)
             if s >= 3 + GAMMA_ON_GPSIMD:
                 apply_gamma_and_store(s - 3, False)
         negative_mean(TILES - 1)
-        finish_last_tile(TILES - 1)
+        sum_of_squares(TILES - 1)
+        scale_from_variance(TILES - 1)
+        centre_and_apply_gamma(TILES - 2)
+        scale_and_store(TILES - 2, nc.scalar)
+        apply_gamma_and_store(TILES - 3, False)
+        centre_and_apply_gamma(TILES - 1)
+        scale_and_store(TILES - 1, nc.vector)

import math
from contextlib import ExitStack

import concourse.mybir as mybir
from concourse.masks import make_identity

F32 = mybir.dt.float32
BF16 = mybir.dt.bfloat16
U32 = mybir.dt.uint32
U8 = mybir.dt.uint8
I32 = mybir.dt.int32
FP8X4 = mybir.dt.float8_e4m3fn_x4
ALU = mybir.AluOpType
ACT = mybir.ActivationFunctionType

P = 128
TOKENS = 1024
D = 1024
CHANNELS = 1024
TILES = TOKENS // P
K_PASS = 4 * P
PASSES = D // K_PASS
HALF = CHANNELS // 2
PAIRS = HALF // 2
DOUBLINGS = 8
assert 2**DOUBLINGS == PAIRS
W_BLOCKS = CHANNELS // (2 * P)
WORDS = D // 2
EPS = 1e-6
THETA_BASE = 100.0
TWO_PI = 2.0 * math.pi
GPSIMD_COLUMNS = 768
GAMMA_ON_GPSIMD = 4
FIRST_COPIED_BY_VECTOR = 6

FLOPS = 2 * TOKENS * D * CHANNELS


def tile_attentionalsplatting_pa_kernel(tc, updated_track_tokens, tracks, W_k, k_gamma, out):
    nc = tc.nc

    x_dram = updated_track_tokens.flatten_outer_dims().rearrange("(p j) k -> p j k", j=TILES)
    pos_dram = tracks.flatten_outer_dims().rearrange("(p j) c -> p (j c)", j=TILES)
    w_dram = W_k.rearrange("(q p e) k -> q p (e k)", q=W_BLOCKS, p=P, e=2)
    out_dram = out.flatten_outer_dims().rearrange("(p j) c -> p j c", j=TILES)

    with ExitStack() as ctx:
        keep = ctx.enter_context(tc.tile_pool(name="keep", bufs=1))
        double = ctx.enter_context(tc.tile_pool(name="double", bufs=2))
        triple = ctx.enter_context(tc.tile_pool(name="triple", bufs=3))
        quad = ctx.enter_context(tc.tile_pool(name="quad", bufs=4))
        stats = ctx.enter_context(tc.tile_pool(name="stats", bufs=6))
        flip_banks = ctx.enter_context(tc.psum_pool(name="flip_banks", bufs=4))
        key_banks = ctx.enter_context(tc.psum_pool(name="key_banks", bufs=2))
        ctx.enter_context(tc.manual_schedule())

        pos_bf = keep.tile([P, 2 * TILES], BF16)
        nc.sync.dma_start(out=pos_bf[:], in_=pos_dram)
        w_raw = keep.tile([P, W_BLOCKS, 2, D], BF16)
        x_raw = keep.tile([P, TILES, D], BF16)

        def load_weights(q):
            nc.sync.dma_start(out=w_raw[:, q].rearrange("p e k -> p (e k)"), in_=w_dram[q])

        def load_tokens(j):
            nc.sync.dma_start(out=x_raw[:, j : j + 2, :], in_=x_dram[:, j : j + 2, :])

        for e in range(2):
            nc.sync.dma_start(out=w_raw[:, 0, e, :], in_=w_dram[0][:, e * D : (e + 1) * D])
        load_weights(1)
        load_tokens(0)
        load_weights(2)
        load_weights(3)
        for j in range(2, TILES, 2):
            load_tokens(j)
        gamma = keep.tile([P, CHANNELS], BF16)
        nc.sync.dma_start(out=gamma[:], in_=k_gamma.partition_broadcast(P))

        ident = keep.tile([P, P], F32)
        make_identity(nc, ident[:])
        minus_half = keep.tile([P, 1], F32)
        nc.gpsimd.memset(minus_half[:], -0.5)
        one = keep.tile([P, 1], F32)
        nc.vector.memset(one[:], 1.0)
        first_sin = keep.tile([P, 1], F32)
        nc.scalar.activation(out=first_sin[:], in_=one[:], func=ACT.Sin)
        theta = keep.tile([P, PAIRS], F32)
        nc.vector.tensor_scalar_mul(out=theta[:, 0:1], in0=one[:], scalar1=1.0 / TWO_PI)
        for w in [2**doubling for doubling in range(DOUBLINGS)]:
            nc.vector.tensor_scalar_mul(
                out=theta[:, w : 2 * w], in0=theta[:, 0:w], scalar1=THETA_BASE ** (-w / PAIRS)
            )
        pos = keep.tile([P, 2 * TILES], F32)
        nc.vector.tensor_copy(out=pos[:], in_=pos_bf[:])
        frac = keep.tile([P, 2 * TILES, PAIRS], F32)

        w_grouped = keep.tile([P, 2, PASSES * HALF * 4], BF16, align_bytes=64)
        w_codes = keep.tile([P, 2, PASSES * HALF], U32, align_bytes=64)
        w_scales = keep.tile([P, 2, PASSES * HALF], U8, align_bytes=64)
        x_grouped = keep.tile([P, TILES, PASSES * P * 4], BF16, align_bytes=64)
        x_codes = keep.tile([P, TILES, PASSES * P], U32, align_bytes=64)
        x_scales = keep.tile([P, TILES, PASSES * P], U8, align_bytes=64)

        trig_of, keys_of, products_of, rotated_of, sums_of, minus_mean_of = {}, {}, {}, {}, {}, {}
        sum_squares_of, rstd_of, shift_of, normed_of, weighted_of = {}, {}, {}, {}, {}

        def flip_rows(words, grouped_words, copy_engine="scalar"):
            bank = flip_banks.tile([P, PASSES * 2 * P], F32, name="flip_bank")
            for t in range(PASSES * 2):
                g, u = divmod(t, 2)
                every_second = words[:, g * 2 * P + u : (g + 1) * 2 * P : 2]
                nc.tensor.transpose(bank[:, t * P : (t + 1) * P], every_second, ident[:])
            planes = bank[:].rearrange("p (g u r) -> p g r u", g=PASSES, u=2)
            if copy_engine == "scalar":
                nc.scalar.copy(out=grouped_words, in_=planes)
            else:
                nc.vector.tensor_copy(out=grouped_words, in_=planes)

        def flip_weights(q):
            h, b = divmod(q, W_BLOCKS // 2)
            half_words = w_grouped[:, h, :].bitcast(F32).rearrange("p (g c u) -> p g c u", g=PASSES, u=2)
            for e in range(2):
                first = e * PAIRS + b * P
                flip_rows(w_raw[:, q, e, :].bitcast(F32), half_words[:, :, first : first + P, :])

        def quantise_weights(h):
            nc.vector.quantize_mx(
                out=w_codes[:, h, :].bitcast(FP8X4), scales=w_scales[:, h, :], in_=w_grouped[:, h, :]
            )

        def flip_tokens(j, copy_engine="scalar"):
            tile_words = x_grouped[:, j, :].bitcast(F32).rearrange("p (g r u) -> p g r u", g=PASSES, u=2)
            flip_rows(x_raw[:, j, :].bitcast(F32), tile_words, copy_engine)

        def quantise_tokens(j):
            nc.vector.quantize_mx(
                out=x_codes[:, j, :].bitcast(FP8X4), scales=x_scales[:, j, :], in_=x_grouped[:, j, :]
            )

        def reduce_angles(j):
            whole = double.tile([P, 2, PAIRS], I32, name="whole")
            for h in range(2):
                nc.vector.tensor_scalar_mul(
                    out=whole[:, h, :], in0=theta[:], scalar1=pos[:, 2 * j + h : 2 * j + h + 1]
                )
            for h in range(2):
                nc.vector.scalar_tensor_tensor(
                    out=frac[:, 2 * j + h, :], in0=theta[:], scalar=pos[:, 2 * j + h : 2 * j + h + 1],
                    in1=whole[:, h, :], op0=ALU.mult, op1=ALU.subtract,
                )

        def cos_and_sin(j):
            tile_frac = frac[:, 2 * j : 2 * j + 2, :].rearrange("p h i -> p (h i)")
            trig_of[j] = quad.tile([P, 2, HALF], F32, name="trig")
            abs_frac = double.tile([P, HALF], F32, name="abs_frac")
            nc.scalar.activation(out=abs_frac[:], in_=tile_frac, func=ACT.Abs)
            nc.scalar.activation(out=trig_of[j][:, 1, :], in_=tile_frac, func=ACT.Sin, scale=TWO_PI)
            nc.scalar.activation(
                out=trig_of[j][:, 0, :], in_=abs_frac[:], func=ACT.Sin, scale=-TWO_PI, bias=math.pi / 2.0
            )

        def project(j, h):
            bank = key_banks.tile([P, HALF], F32, name="key_bank_%d" % h)
            for g in range(PASSES):
                nc.tensor.matmul_mx(
                    out=bank[:],
                    lhsT=x_codes[:, j, g * P : (g + 1) * P].bitcast(FP8X4),
                    lhsT_scale=x_scales[:, j, g * P : (g + 1) * P],
                    rhs=w_codes[:, h, g * HALF : (g + 1) * HALF].bitcast(FP8X4),
                    rhs_scale=w_scales[:, h, g * HALF : (g + 1) * HALF],
                    start=(g == 0),
                    stop=(g == PASSES - 1),
                )
            keys_of[j, h] = bank

        def multiply(j, h):
            if h == 0:
                products_of[j] = triple.tile([P, 2, 2, 2, PAIRS], F32, name="work")
            planes = keys_of[j, h][:].rearrange("p (e i) -> p e i", e=2)
            nc.vector.tensor_mul(
                out=products_of[j][:, h],
                in0=planes.unsqueeze(1).to_broadcast([P, 2, 2, PAIRS]),
                in1=trig_of[j][:, :, h * PAIRS : (h + 1) * PAIRS].unsqueeze(2).to_broadcast([P, 2, 2, PAIRS]),
            )

        def add_products(j):
            products = products_of[j]
            rotated_of[j] = quad.tile([P, 2, 2, PAIRS], F32, name="rotated")
            sums_of[j] = stats.tile([P, 2], F32, name="sums")
            nc.vector.scalar_tensor_tensor(
                out=rotated_of[j][:, :, 0, :], in0=products[:, :, 0, 0, :], scalar=1.0, in1=products[:, :, 1, 1, :],
                op0=ALU.mult, op1=ALU.subtract, accum_out=sums_of[j][:, 0:1],
            )
            nc.vector.scalar_tensor_tensor(
                out=rotated_of[j][:, :, 1, :], in0=products[:, :, 0, 1, :], scalar=1.0, in1=products[:, :, 1, 0, :],
                op0=ALU.mult, op1=ALU.add, accum_out=sums_of[j][:, 1:2],
            )

        def negative_mean(j):
            scaled = stats.tile([P, 2], F32, name="scaled")
            minus_mean_of[j] = stats.tile([P, 1], F32, name="minus_mean")
            nc.scalar.activation(
                out=scaled[:], in_=sums_of[j][:], func=ACT.Copy, scale=-1.0 / CHANNELS, accum_out=minus_mean_of[j][:]
            )

        def sum_of_squares(j):
            squares = double.tile([P, CHANNELS], F32, name="squares")
            sum_squares_of[j] = stats.tile([P, 1], F32, name="sum_squares")
            nc.scalar.activation(
                out=squares[:], in_=rotated_of[j][:].rearrange("p h e i -> p (h e i)"), func=ACT.Square,
                bias=minus_mean_of[j][:], scale=1.0, accum_out=sum_squares_of[j][:],
            )

        def scale_from_variance(j):
            var_eps = stats.tile([P, 1], F32, name="var_eps")
            nc.gpsimd.tensor_scalar(
                out=var_eps[:], in0=sum_squares_of[j][:], scalar1=1.0 / CHANNELS, scalar2=EPS,
                op0=ALU.mult, op1=ALU.add,
            )
            rstd_of[j] = stats.tile([P, 1], F32, name="rstd")
            nc.gpsimd.tensor_tensor(out=rstd_of[j][:], in0=var_eps[:], in1=minus_half[:], op=ALU.pow)

        def shift_from_scale(j):
            shift_of[j] = stats.tile([P, 1], F32, name="shift")
            nc.scalar.activation(out=shift_of[j][:], in_=minus_mean_of[j][:], func=ACT.Copy, scale=rstd_of[j][:])

        def normalise(j):
            normed_of[j] = triple.tile([P, CHANNELS], F32, name="normed")
            nc.scalar.activation(
                out=normed_of[j][:].rearrange("p (h i e) -> p h i e", h=2, e=2),
                in_=rotated_of[j][:].rearrange("p h e i -> p h i e"),
                func=ACT.Identity, bias=shift_of[j][:], scale=rstd_of[j][:],
            )

        def apply_gamma_and_store(j, shared):
            if shared:
                result = triple.tile([P, CHANNELS], F32, name="work")
                nc.gpsimd.tensor_tensor(
                    out=result[:, 0:GPSIMD_COLUMNS], in0=normed_of[j][:, 0:GPSIMD_COLUMNS], in1=gamma[:, 0:GPSIMD_COLUMNS], op=ALU.mult
                )
                nc.vector.tensor_tensor(
                    out=result[:, GPSIMD_COLUMNS:], in0=normed_of[j][:, GPSIMD_COLUMNS:], in1=gamma[:, GPSIMD_COLUMNS:], op=ALU.mult
                )
            else:
                result = triple.tile([P, CHANNELS], F32, name="result")
                nc.vector.tensor_tensor(out=result[:], in0=normed_of[j][:], in1=gamma[:], op=ALU.mult)
            nc.sync.dma_start(out=out_dram[:, j, :], in_=result[:])

        def centre_and_apply_gamma(j):
            weighted_of[j] = keep.tile([P, CHANNELS], F32, name="weighted_%d" % j)
            for h in range(2):
                columns = slice(h * HALF, (h + 1) * HALF)
                nc.vector.scalar_tensor_tensor(
                    out=weighted_of[j][:, columns].rearrange("p (i e) -> p i e", e=2),
                    in0=rotated_of[j][:, h].rearrange("p e i -> p i e"),
                    scalar=minus_mean_of[j][:],
                    in1=gamma[:, columns].rearrange("p (i e) -> p i e", e=2),
                    op0=ALU.add, op1=ALU.mult,
                )

        def scale_and_store(j, engine):
            for h in range(2):
                columns = slice(h * HALF, (h + 1) * HALF)
                result = quad.tile([P, HALF], F32, name="half_result")
                if engine is nc.scalar:
                    nc.scalar.activation(
                        out=result[:], in_=weighted_of[j][:, columns], func=ACT.Copy, scale=rstd_of[j][:]
                    )
                else:
                    nc.vector.tensor_scalar_mul(out=result[:], in0=weighted_of[j][:, columns], scalar1=rstd_of[j][:])
                nc.sync.dma_start(out=out_dram[:, j, columns], in_=result[:])

        reduce_angles(0)
        reduce_angles(1)
        cos_and_sin(0)
        flip_weights(0)
        reduce_angles(2)
        reduce_angles(3)
        reduce_angles(4)
        reduce_angles(5)
        flip_weights(1)
        flip_tokens(0)
        quantise_weights(0)
        quantise_tokens(0)
        flip_weights(2)
        reduce_angles(6)
        reduce_angles(7)
        flip_weights(3)
        flip_tokens(1)
        project(0, 0)
        quantise_weights(1)
        multiply(0, 0)
        cos_and_sin(1)
        flip_tokens(2)
        project(0, 1)
        quantise_tokens(1)

        for s in range(TILES):
            if s >= 1:
                negative_mean(s - 1)
            if s + 3 < TILES:
                flip_tokens(s + 3, "scalar" if s + 3 < FIRST_COPIED_BY_VECTOR else "vector")
            if s + 1 < TILES:
                project(s + 1, 0)
                project(s + 1, 1)
            if s > 0:
                multiply(s, 0)
            multiply(s, 1)
            if s >= 1:
                sum_of_squares(s - 1)
            if s >= 2:
                shift_from_scale(s - 2)
                normalise(s - 2)
            if s + 2 < TILES:
                quantise_tokens(s + 2)
                cos_and_sin(s + 2)
            if 3 <= s < 3 + GAMMA_ON_GPSIMD:
                apply_gamma_and_store(s - 3, True)
            if s >= 1:
                scale_from_variance(s - 1)
            add_products(s)
            if s >= 3 + GAMMA_ON_GPSIMD:
                apply_gamma_and_store(s - 3, False)
        negative_mean(TILES - 1)
        sum_of_squares(TILES - 1)
        scale_from_variance(TILES - 1)
        centre_and_apply_gamma(TILES - 2)
        scale_and_store(TILES - 2, nc.scalar)
        apply_gamma_and_store(TILES - 3, False)
        centre_and_apply_gamma(TILES - 1)
        scale_and_store(TILES - 1, nc.vector)
